import numpy as np
import ml_dtypes


def mxq(x, axis, fmt="e4m3"):
    dtype, down = {"e4m3": (ml_dtypes.float8_e4m3fn, 7), "e5m2": (ml_dtypes.float8_e5m2, 14)}[fmt]
    v = np.moveaxis(np.asarray(x, np.float32).astype(ml_dtypes.bfloat16).astype(np.float64), axis, -1)
    blocks = v.reshape(v.shape[:-1] + (-1, 32))
    amax = np.abs(blocks).max(-1, keepdims=True)
    byte = np.maximum(np.where(amax > 0, np.frexp(amax)[1] - 1 + 127, 0) - down, 1)
    scale = np.exp2(byte - 127.0)
    codes = (blocks / scale).astype(np.float32).astype(dtype).astype(np.float64)
    return np.moveaxis((codes * scale).reshape(v.shape), -1, axis)


WIDE = False


def mx_kscale(k):
    if not WIDE:
        return np.ones(k)
    levels = np.array([10, -10, 5, -5, 0])
    a = np.random.permutation(np.resize(levels, k // 512 * 4)).reshape(k // 512, 4)
    idx = np.arange(k)
    return np.exp2(a[idx // 512, idx % 128 // 32])


BF16 = ml_dtypes.bfloat16


def bf(x):
    return np.asarray(x, np.float32).astype(BF16)


def f64(x):
    return np.asarray(x).astype(np.float64)


E2M1 = np.array([0.0, 0.5, 1.0, 1.5, 2.0, 3.0, 4.0, 6.0, -0.0, -0.5, -1.0, -1.5, -2.0, -3.0, -4.0, -6.0])


def pack_weight(w, fmt):
    k, n = w.shape
    w = f64(bf(w)).reshape(k // 32, 32, n)
    amax = np.abs(w).max(1)
    if fmt == "e4m3":
        byte = np.frexp(amax)[1] - 1 + 127 - 7
    else:
        mant, ex = np.frexp(amax / 6.0)
        byte = np.where(mant > 0.5, ex, ex - 1) + 127
    byte = np.clip(np.where(amax > 0, byte, 1), 1, 254)
    scaled = (w * np.exp2(127.0 - byte)[:, None, :]).reshape(k, n).astype(np.float32)
    by_word = np.ascontiguousarray(scaled.reshape(k // 512, 128, 4, n).transpose(0, 1, 3, 2))
    if fmt == "e4m3":
        words = by_word.astype(ml_dtypes.float8_e4m3fn).view(np.uint8)
    else:
        c = by_word.astype(ml_dtypes.float4_e2m1fn).view(np.uint8) & 0xF
        words = c[..., 0::2] | (c[..., 1::2] << 4)
    return np.ascontiguousarray(words), np.ascontiguousarray(byte.astype(np.uint8).reshape(k // 512, 16, n))


def unpack_weight(words, scales, fmt):
    g, p, n, _ = words.shape
    if fmt == "e4m3":
        vals = np.ascontiguousarray(words).view(ml_dtypes.float8_e4m3fn).astype(np.float64)
    else:
        nib = np.empty((g, p, n, 4), np.uint8)
        nib[..., 0::2] = words & 0xF
        nib[..., 1::2] = words >> 4
        vals = E2M1[nib]
    vals = vals * np.repeat(np.exp2(scales.astype(np.float64) - 127.0), 8, axis=1)[..., None]
    return vals.transpose(0, 1, 3, 2).reshape(g * 512, n)


B, N, F, O, E, K = 16, 512, 512, 16, 16, 3


def setup_inputs():
    s = mx_kscale(F)
    x_g = bf(np.random.standard_normal((B, K, N, F)) * s)
    emb = bf(np.random.standard_normal((B, N, E)))
    stack = np.random.standard_normal((E, K, F, O)) * 0.5 / np.sqrt(K * F) / s[:, None]
    words, scales = pack_weight(stack.reshape(-1, O), "e4m3")
    bias_pool = bf(np.random.standard_normal((E, O)) * 0.3)
    return {"x_g": x_g,
            "emb": emb,
            "weights_pool_words": words,
            "weights_pool_scales": scales,
            "bias_pool": bias_pool}


def reference(x_g, emb, weights_pool_words, weights_pool_scales, bias_pool):
    xg, g = f64(x_g), f64(emb)
    w = unpack_weight(weights_pool_words, weights_pool_scales, "e4m3").reshape(E, K, F, O)
    z = 0.0
    for k in range(K):
        wk = w[:, k].transpose(1, 0, 2).reshape(F, E * O)
        z = z + (mxq(xg[:, k], 2, "e4m3") @ wk)
    z = z.reshape(B, N, E, O)
    out = (g[:, :, :, None] * z).sum(2)
    return out + (g[:, :, :, None] * f64(bias_pool)[None, None, :, :]).sum(2)

@@ -1,0 +1,209 @@
+from contextlib import ExitStack
+
+import concourse.mybir as mybir
+from concourse.masks import make_identity
+
+BF16 = mybir.dt.bfloat16
+F32 = mybir.dt.float32
+I32 = mybir.dt.int32
+U8 = mybir.dt.uint8
+FP8X4 = mybir.dt.float8_e4m3fn_x4
+MULT = mybir.AluOpType.mult
+ADD = mybir.AluOpType.add
+
+B, J, N, F, E, O = 16, 3, 512, 512, 16, 16
+P = 128
+PACK = 4
+HALVES = 2
+TILES = N // P
+EO = E * O
+ROUND_TILES = 2
+ROUNDS_PER_BATCH = TILES // ROUND_TILES
+ROUNDS = B * ROUNDS_PER_BATCH
+AHEAD = 2
+X_BUFS = 4
+CHUNK_TILES = P // E
+CHUNKS = B * TILES // CHUNK_TILES
+
+FLOPS = 2 * B * N * J * F * EO + 4 * B * N * EO
+
+
+def tile_dygcn_pb_t_e_kernel(
+    tc, x_g, emb, weights_pool_words, weights_pool_scales, bias_pool, out
+):
+    nc = tc.nc
+    with ExitStack() as ctx:
+        const = ctx.enter_context(tc.tile_pool(name="const", bufs=1))
+        x_pool = ctx.enter_context(tc.tile_pool(name="x", bufs=X_BUFS))
+        stage = ctx.enter_context(tc.tile_pool(name="stage", bufs=3))
+        mx_pool = ctx.enter_context(tc.tile_pool(name="mx", bufs=AHEAD + 2))
+        psum_t = ctx.enter_context(tc.psum_pool(name="psum_t", bufs=6))
+        psum_z = ctx.enter_context(tc.psum_pool(name="psum_z", bufs=2))
+        ctx.enter_context(tc.manual_schedule())
+
+        x_tiles = {}
+        mx_tiles = {}
+        res_tiles = {}
+
+        def load_batch(b):
+            x_sb = x_pool.tile([P, J, TILES, F], BF16, name="x_sb")
+            for j in range(J):
+                nc.sync.dma_start(
+                    out=x_sb[:, j], in_=x_g[b, j].rearrange("(p t) f -> p t f", t=TILES)
+                )
+            x_tiles[b] = x_sb
+
+        def transpose_round(r):
+            b, first = r // ROUNDS_PER_BATCH, (r % ROUNDS_PER_BATCH) * ROUND_TILES
+            words = x_tiles[b][:].bitcast(F32)
+            grouped = stage.tile([P, J, ROUND_TILES, P, PACK], BF16, name="grouped", align_bytes=64)
+            codes = mx_pool.tile([P, J, ROUND_TILES * P], I32, name="codes", align_bytes=64)
+            scales = mx_pool.tile([P, J, ROUND_TILES * P], U8, name="scales", align_bytes=64)
+            for j in range(J):
+                flipped = psum_t.tile([P, ROUND_TILES, HALVES, P], F32, name="flipped", tag="t")
+                for t in range(ROUND_TILES):
+                    for u in range(HALVES):
+                        nc.tensor.transpose(
+                            flipped[:, t, u, :], words[:, j, first + t, u : F // 2 : HALVES], ident_f32[:]
+                        )
+                nc.scalar.copy(
+                    out=grouped[:].bitcast(F32)[:, j],
+                    in_=flipped[:].rearrange("p t u c -> p t c u"),
+                )
+                nc.vector.quantize_mx(
+                    out=codes[:, j, :].bitcast(FP8X4),
+                    scales=scales[:, j, :],
+                    in_=grouped[:, j].rearrange("p t c k -> p (t c k)"),
+                )
+            mx_tiles[r] = (codes, scales)
+            if first + ROUND_TILES == TILES and b + X_BUFS < B:
+                load_batch(b + X_BUFS)
+
+        def multiply_round(r):
+            b, first = r // ROUNDS_PER_BATCH, (r % ROUNDS_PER_BATCH) * ROUND_TILES
+            codes, scales = mx_tiles.pop(r)
+            z = psum_z.tile([P, ROUND_TILES, EO], F32, name="z", tag="z")
+            for t in range(ROUND_TILES):
+                nodes = slice(t * P, (t + 1) * P)
+                for j in range(J):
+                    nc.tensor.matmul_mx(
+                        out=z[:, t, :],
+                        lhsT=codes[:, j, nodes].bitcast(FP8X4),
+                        lhsT_scale=scales[:, j, nodes],
+                        rhs=w_codes[:, j, :].bitcast(FP8X4),
+                        rhs_scale=w_scales[:, j, :],
+                        start=(j == 0),
+                        stop=(j == J - 1),
+                    )
+            weighted = stage.tile([P, ROUND_TILES, E, O], F32, name="weighted")
+            nc.vector.tensor_tensor(
+                out=weighted[:],
+                in0=z[:].rearrange("p t (e o) -> p t e o", o=O),
+                in1=emb_sb[:, b, first : first + ROUND_TILES, :]
+                .unsqueeze(3)
+                .to_broadcast([P, ROUND_TILES, E, O]),
+                op=MULT,
+            )
+            if first == 0:
+                res_tiles[b] = stage.tile([P, TILES, O], F32, name="res")
+            res = res_tiles[b]
+            nc.vector.tensor_reduce(
+                out=res[:, first : first + ROUND_TILES, :],
+                in_=weighted[:].rearrange("p t e o -> p t o e"),
+                axis=mybir.AxisListType.X,
+                op=ADD,
+            )
+            if first + ROUND_TILES == TILES:
+                nc.vector.tensor_tensor(out=res[:], in0=res[:], in1=bias_term[:, b], op=ADD)
+                nc.sync.dma_start(
+                    out=out[b].rearrange("(p t) o -> p t o", t=TILES), in_=res_tiles.pop(b)[:]
+                )
+
+        ident_f32 = const.tile([P, P], F32, name="ident_f32")
+        make_identity(nc, ident_f32[:])
+        ident_bf16 = const.tile([P, P], BF16, name="ident_bf16")
+        make_identity(nc, ident_bf16[:])
+
+        load_batch(0)
+
+        emb_sb = const.tile([P, B, TILES, E], BF16, name="emb_sb")
+        nc.sync.dma_start(out=emb_sb[:], in_=emb.rearrange("b (p t) e -> p b t e", t=TILES))
+        bias_rows = const.tile([P, O], BF16, name="bias_rows")
+        nc.sync.dma_start(
+            out=bias_rows[:], in_=bias_pool.unsqueeze(0).to_broadcast([CHUNK_TILES, E, O])
+        )
+
+        w_scales_in = const.tile([P, E * J * O], U8, name="w_scales_in")
+        nc.vector.memset(w_scales_in[:].bitcast(I32), 0)
+        scale_rows = weights_pool_scales.bitcast(I32).rearrange("g (q r) w -> q r g w", r=4)
+        for q in range(4):
+            nc.sync.dma_start(
+                out=w_scales_in[32 * q : 32 * q + 4, :]
+                .bitcast(I32)
+                .rearrange("r (g w) -> r g w", w=O // 4),
+                in_=scale_rows[q],
+            )
+        w_codes = const.tile([P, J, EO], I32, name="w_codes", align_bytes=64)
+        code_words = (
+            weights_pool_words.rearrange("g p n t -> g p (n t)")
+            .bitcast(I32)
+            .rearrange("(e j) p n -> j p e n", j=J)
+        )
+        for j in range(J):
+            nc.sync.dma_start(
+                out=w_codes[:, j, :].rearrange("p (e n) -> p e n", n=O), in_=code_words[j]
+            )
+        for b in range(1, X_BUFS):
+            load_batch(b)
+
+        for r in range(AHEAD):
+            transpose_round(r)
+
+        same_tile = const.tile([P, CHUNK_TILES], F32, name="same_tile")
+        nc.vector.tensor_reduce(
+            out=same_tile[:],
+            in_=ident_bf16[:].rearrange("p (i e) -> p i e", e=E),
+            axis=mybir.AxisListType.X,
+            op=ADD,
+        )
+        bias_blocks = const.tile([P, CHUNK_TILES, O], BF16, name="bias_blocks")
+        nc.vector.tensor_tensor(
+            out=bias_blocks[:],
+            in0=bias_rows[:].unsqueeze(1).to_broadcast([P, CHUNK_TILES, O]),
+            in1=same_tile[:].unsqueeze(2).to_broadcast([P, CHUNK_TILES, O]),
+            op=MULT,
+        )
+        emb_cols = emb_sb[:].rearrange("p b t e -> p (b t e)")
+        emb_flipped = psum_t.tile([P, CHUNKS, P], BF16, name="emb_flipped", tag="t")
+        for c in range(CHUNKS):
+            nc.tensor.transpose(emb_flipped[:, c, :], emb_cols[:, c * P : (c + 1) * P], ident_bf16[:])
+        emb_t = const.tile([P, CHUNKS, P], BF16, name="emb_t")
+        nc.vector.tensor_copy(out=emb_t[:], in_=emb_flipped[:])
+        bias_term = const.tile([P, B, TILES, O], F32, name="bias_term")
+        bias_term_cols = bias_term[:].rearrange("p b t o -> p (b t o)")
+        bank_chunks = 512 // P
+        for half in range(CHUNKS // bank_chunks):
+            product = psum_z.tile([P, bank_chunks, P], F32, name="product", tag="z")
+            for i in range(bank_chunks):
+                nc.tensor.matmul(
+                    out=product[:, i, :],
+                    lhsT=emb_t[:, half * bank_chunks + i, :],
+                    rhs=bias_blocks[:].rearrange("p i o -> p (i o)"),
+                    start=True,
+                    stop=True,
+                )
+            nc.vector.tensor_copy(
+                out=bias_term_cols[:, half * 512 : (half + 1) * 512],
+                in_=product[:].rearrange("p i c -> p (i c)"),
+            )
+
+        w_scales = const.tile([P, J, EO], U8, name="w_scales", align_bytes=64)
+        nc.vector.tensor_copy(
+            out=w_scales[:].bitcast(I32).rearrange("p j (e w) -> p j e w", w=O // 4),
+            in_=w_scales_in[:].bitcast(I32).rearrange("p (e j w) -> p j e w", j=J, w=O // 4),
+        )
+
+        for r in range(ROUNDS):
+            multiply_round(r)
+            if r + AHEAD < ROUNDS:
+                transpose_round(r + AHEAD)

@@ -17,8 +17,10 @@ PACK = 4
 HALVES = 2
 TILES = N // P
 EO = E * O
-ROUND_TILES = 2
-ROUNDS_PER_BATCH = TILES // ROUND_TILES
+BANK_UNITS = 2
+BANK_TILES = 2
+ROUND_UNITS = 4
+ROUNDS_PER_BATCH = TILES * J // ROUND_UNITS
 ROUNDS = B * ROUNDS_PER_BATCH
 AHEAD = 2
 X_BUFS = 4
@@ -43,7 +45,13 @@ def tile_dygcn_pb_t_e_kernel(
 
         x_tiles = {}
         mx_tiles = {}
+        z_tiles = {}
         res_tiles = {}
+
+        def unit_of(r, k):
+            tile_index, j = divmod(r * ROUND_UNITS + k, J)
+            b, t = divmod(tile_index, TILES)
+            return b, t, j
 
         def load_batch(b):
             x_sb = x_pool.tile([P, J, TILES, F], BF16, name="x_sb")
@@ -54,66 +62,68 @@ def tile_dygcn_pb_t_e_kernel(
             x_tiles[b] = x_sb
 
         def transpose_round(r):
-            b, first = r // ROUNDS_PER_BATCH, (r % ROUNDS_PER_BATCH) * ROUND_TILES
-            words = x_tiles[b][:].bitcast(F32)
-            grouped = stage.tile([P, J, ROUND_TILES, P, PACK], BF16, name="grouped", align_bytes=64)
-            codes = mx_pool.tile([P, J, ROUND_TILES * P], I32, name="codes", align_bytes=64)
-            scales = mx_pool.tile([P, J, ROUND_TILES * P], U8, name="scales", align_bytes=64)
-            for j in range(J):
-                flipped = psum_t.tile([P, ROUND_TILES, HALVES, P], F32, name="flipped", tag="t")
-                for t in range(ROUND_TILES):
+            grouped = stage.tile([P, ROUND_UNITS, P, PACK], BF16, name="grouped", align_bytes=64)
+            codes = mx_pool.tile([P, ROUND_UNITS * P], I32, name="codes", align_bytes=64)
+            scales = mx_pool.tile([P, ROUND_UNITS * P], U8, name="scales", align_bytes=64)
+            for first in range(0, ROUND_UNITS, BANK_UNITS):
+                flipped = psum_t.tile([P, BANK_UNITS, HALVES, P], F32, name="flipped", tag="t")
+                for i in range(BANK_UNITS):
+                    b, t, j = unit_of(r, first + i)
+                    words = x_tiles[b][:].bitcast(F32)
                     for u in range(HALVES):
                         nc.tensor.transpose(
-                            flipped[:, t, u, :], words[:, j, first + t, u : F // 2 : HALVES], ident_f32[:]
+                            flipped[:, i, u, :], words[:, j, t, u : F // 2 : HALVES], ident_f32[:]
                         )
                 nc.scalar.copy(
-                    out=grouped[:].bitcast(F32)[:, j],
-                    in_=flipped[:].rearrange("p t u c -> p t c u"),
+                    out=grouped[:].bitcast(F32)[:, first : first + BANK_UNITS],
+                    in_=flipped[:].rearrange("p i u c -> p i c u"),
                 )
-                nc.vector.quantize_mx(
-                    out=codes[:, j, :].bitcast(FP8X4),
-                    scales=scales[:, j, :],
-                    in_=grouped[:, j].rearrange("p t c k -> p (t c k)"),
-                )
+            nc.vector.quantize_mx(
+                out=codes[:].bitcast(FP8X4),
+                scales=scales[:],
+                in_=grouped[:].rearrange("p i c k -> p (i c k)"),
+            )
             mx_tiles[r] = (codes, scales)
-            if first + ROUND_TILES == TILES and b + X_BUFS < B:
+            b = r // ROUNDS_PER_BATCH
+            if (r + 1) % ROUNDS_PER_BATCH == 0 and b + X_BUFS < B:
                 load_batch(b + X_BUFS)
 
         def multiply_round(r):
-            b, first = r // ROUNDS_PER_BATCH, (r % ROUNDS_PER_BATCH) * ROUND_TILES
             codes, scales = mx_tiles.pop(r)
-            z = psum_z.tile([P, ROUND_TILES, EO], F32, name="z", tag="z")
-            for t in range(ROUND_TILES):
-                nodes = slice(t * P, (t + 1) * P)
-                for j in range(J):
-                    nc.tensor.matmul_mx(
-                        out=z[:, t, :],
-                        lhsT=codes[:, j, nodes].bitcast(FP8X4),
-                        lhsT_scale=scales[:, j, nodes],
-                        rhs=w_codes[:, j, :].bitcast(FP8X4),
-                        rhs_scale=w_scales[:, j, :],
-                        start=(j == 0),
-                        stop=(j == J - 1),
-                    )
-            weighted = stage.tile([P, ROUND_TILES, E, O], F32, name="weighted")
+            for k in range(ROUND_UNITS):
+                b, t, j = unit_of(r, k)
+                pair, side = divmod(t, BANK_TILES)
+                if side == 0 and j == 0:
+                    z_tiles[b, pair] = psum_z.tile([P, BANK_TILES, EO], F32, name="z", tag="z")
+                nodes = slice(k * P, (k + 1) * P)
+                nc.tensor.matmul_mx(
+                    out=z_tiles[b, pair][:, side, :],
+                    lhsT=codes[:, nodes].bitcast(FP8X4),
+                    lhsT_scale=scales[:, nodes],
+                    rhs=w_codes[:, j, :].bitcast(FP8X4),
+                    rhs_scale=w_scales[:, j, :],
+                    start=(j == 0),
+                    stop=(j == J - 1),
+                )
+                if side == BANK_TILES - 1 and j == J - 1:
+                    finish_pair(b, pair)
+
+        def finish_pair(b, pair):
+            tiles = slice(pair * BANK_TILES, (pair + 1) * BANK_TILES)
+            weighted = stage.tile([P, BANK_TILES, O, E], F32, name="weighted")
             nc.vector.tensor_tensor(
                 out=weighted[:],
-                in0=z[:].rearrange("p t (e o) -> p t e o", o=O),
-                in1=emb_sb[:, b, first : first + ROUND_TILES, :]
-                .unsqueeze(3)
-                .to_broadcast([P, ROUND_TILES, E, O]),
+                in0=z_tiles.pop((b, pair))[:].rearrange("p t (e o) -> p t o e", o=O),
+                in1=emb_sb[:, b, tiles, :].unsqueeze(2).to_broadcast([P, BANK_TILES, O, E]),
                 op=MULT,
             )
-            if first == 0:
+            if pair == 0:
                 res_tiles[b] = stage.tile([P, TILES, O], F32, name="res")
             res = res_tiles[b]
             nc.vector.tensor_reduce(
-                out=res[:, first : first + ROUND_TILES, :],
-                in_=weighted[:].rearrange("p t e o -> p t o e"),
-                axis=mybir.AxisListType.X,
-                op=ADD,
+                out=res[:, tiles, :], in_=weighted[:], axis=mybir.AxisListType.X, op=ADD
             )
-            if first + ROUND_TILES == TILES:
+            if (pair + 1) * BANK_TILES == TILES:
                 nc.vector.tensor_tensor(out=res[:], in0=res[:], in1=bias_term[:, b], op=ADD)
                 nc.sync.dma_start(
                     out=out[b].rearrange("(p t) o -> p t o", t=TILES), in_=res_tiles.pop(b)[:]

@@ -22,7 +22,7 @@ BANK_TILES = 2
 ROUND_UNITS = 4
 ROUNDS_PER_BATCH = TILES * J // ROUND_UNITS
 ROUNDS = B * ROUNDS_PER_BATCH
-AHEAD = 2
+AHEAD = 3
 X_BUFS = 4
 CHUNK_TILES = P // E
 CHUNKS = B * TILES // CHUNK_TILES

@@ -24,6 +24,7 @@ ROUNDS_PER_BATCH = TILES * J // ROUND_UNITS
 ROUNDS = B * ROUNDS_PER_BATCH
 AHEAD = 3
 X_BUFS = 4
+SORTED_ORDERS = 2
 CHUNK_TILES = P // E
 CHUNKS = B * TILES // CHUNK_TILES
 
@@ -37,6 +38,7 @@ def tile_dygcn_pb_t_e_kernel(
     with ExitStack() as ctx:
         const = ctx.enter_context(tc.tile_pool(name="const", bufs=1))
         x_pool = ctx.enter_context(tc.tile_pool(name="x", bufs=X_BUFS))
+        sort_pool = ctx.enter_context(tc.tile_pool(name="sort", bufs=2))
         stage = ctx.enter_context(tc.tile_pool(name="stage", bufs=3))
         mx_pool = ctx.enter_context(tc.tile_pool(name="mx", bufs=AHEAD + 2))
         psum_t = ctx.enter_context(tc.psum_pool(name="psum_t", bufs=6))
@@ -44,6 +46,7 @@ def tile_dygcn_pb_t_e_kernel(
         ctx.enter_context(tc.manual_schedule())
 
         x_tiles = {}
+        sorted_tiles = {}
         mx_tiles = {}
         z_tiles = {}
         res_tiles = {}
@@ -61,6 +64,18 @@ def tile_dygcn_pb_t_e_kernel(
                 )
             x_tiles[b] = x_sb
 
+        def sort_batch(b):
+            words = x_tiles[b][:].bitcast(F32)
+            by_scalar = sort_pool.tile([P, TILES, HALVES, P], F32, name="by_scalar")
+            nc.scalar.copy(
+                out=by_scalar[:], in_=words[:, 0].rearrange("p t (q u) -> p t u q", u=HALVES)
+            )
+            by_vector = sort_pool.tile([P, TILES, HALVES, P], F32, name="by_vector")
+            nc.vector.tensor_copy(
+                out=by_vector[:], in_=words[:, 1].rearrange("p t (q u) -> p t u q", u=HALVES)
+            )
+            sorted_tiles[b] = (by_scalar, by_vector)
+
         def transpose_round(r):
             grouped = stage.tile([P, ROUND_UNITS, P, PACK], BF16, name="grouped", align_bytes=64)
             codes = mx_pool.tile([P, ROUND_UNITS * P], I32, name="codes", align_bytes=64)
@@ -71,9 +86,11 @@ def tile_dygcn_pb_t_e_kernel(
                     b, t, j = unit_of(r, first + i)
                     words = x_tiles[b][:].bitcast(F32)
                     for u in range(HALVES):
-                        nc.tensor.transpose(
-                            flipped[:, i, u, :], words[:, j, t, u : F // 2 : HALVES], ident_f32[:]
-                        )
+                        if j < SORTED_ORDERS:
+                            run = sorted_tiles[b][j][:, t, u, :]
+                        else:
+                            run = words[:, j, t, u : F // 2 : HALVES]
+                        nc.tensor.transpose(flipped[:, i, u, :], run, ident_f32[:])
                 nc.scalar.copy(
                     out=grouped[:].bitcast(F32)[:, first : first + BANK_UNITS],
                     in_=flipped[:].rearrange("p i u c -> p i c u"),
@@ -85,6 +102,8 @@ def tile_dygcn_pb_t_e_kernel(
             )
             mx_tiles[r] = (codes, scales)
             b = r // ROUNDS_PER_BATCH
+            if r % ROUNDS_PER_BATCH == 0 and b + 1 < B:
+                sort_batch(b + 1)
             if (r + 1) % ROUNDS_PER_BATCH == 0 and b + X_BUFS < B:
                 load_batch(b + X_BUFS)
 
@@ -166,6 +185,7 @@ def tile_dygcn_pb_t_e_kernel(
         for b in range(1, X_BUFS):
             load_batch(b)
 
+        sort_batch(0)
         for r in range(AHEAD):
             transpose_round(r)
 

@@ -24,7 +24,7 @@ ROUNDS_PER_BATCH = TILES * J // ROUND_UNITS
 ROUNDS = B * ROUNDS_PER_BATCH
 AHEAD = 3
 X_BUFS = 4
-SORTED_ORDERS = 2
+SORTED_ORDERS = 1
 CHUNK_TILES = P // E
 CHUNKS = B * TILES // CHUNK_TILES
 
@@ -38,7 +38,7 @@ def tile_dygcn_pb_t_e_kernel(
     with ExitStack() as ctx:
         const = ctx.enter_context(tc.tile_pool(name="const", bufs=1))
         x_pool = ctx.enter_context(tc.tile_pool(name="x", bufs=X_BUFS))
-        sort_pool = ctx.enter_context(tc.tile_pool(name="sort", bufs=2))
+        sort_pool = ctx.enter_context(tc.tile_pool(name="sort", bufs=6))
         stage = ctx.enter_context(tc.tile_pool(name="stage", bufs=3))
         mx_pool = ctx.enter_context(tc.tile_pool(name="mx", bufs=AHEAD + 2))
         psum_t = ctx.enter_context(tc.psum_pool(name="psum_t", bufs=6))
@@ -64,19 +64,20 @@ def tile_dygcn_pb_t_e_kernel(
                 )
             x_tiles[b] = x_sb
 
-        def sort_batch(b):
-            words = x_tiles[b][:].bitcast(F32)
-            by_scalar = sort_pool.tile([P, TILES, HALVES, P], F32, name="by_scalar")
-            nc.scalar.copy(
-                out=by_scalar[:], in_=words[:, 0].rearrange("p t (q u) -> p t u q", u=HALVES)
-            )
-            by_vector = sort_pool.tile([P, TILES, HALVES, P], F32, name="by_vector")
-            nc.vector.tensor_copy(
-                out=by_vector[:], in_=words[:, 1].rearrange("p t (q u) -> p t u q", u=HALVES)
-            )
-            sorted_tiles[b] = (by_scalar, by_vector)
+        def sort_round(r):
+            for k in range(ROUND_UNITS):
+                b, t, j = unit_of(r, k)
+                if j < SORTED_ORDERS:
+                    runs = sort_pool.tile([P, HALVES, P], F32, name="runs")
+                    nc.scalar.copy(
+                        out=runs[:],
+                        in_=x_tiles[b][:].bitcast(F32)[:, j, t].rearrange("p (q u) -> p u q", u=HALVES),
+                    )
+                    sorted_tiles[b, t, j] = runs
 
         def transpose_round(r):
+            if r + 1 < ROUNDS:
+                sort_round(r + 1)
             grouped = stage.tile([P, ROUND_UNITS, P, PACK], BF16, name="grouped", align_bytes=64)
             codes = mx_pool.tile([P, ROUND_UNITS * P], I32, name="codes", align_bytes=64)
             scales = mx_pool.tile([P, ROUND_UNITS * P], U8, name="scales", align_bytes=64)
@@ -87,7 +88,7 @@ def tile_dygcn_pb_t_e_kernel(
                     words = x_tiles[b][:].bitcast(F32)
                     for u in range(HALVES):
                         if j < SORTED_ORDERS:
-                            run = sorted_tiles[b][j][:, t, u, :]
+                            run = sorted_tiles[b, t, j][:, u, :]
                         else:
                             run = words[:, j, t, u : F // 2 : HALVES]
                         nc.tensor.transpose(flipped[:, i, u, :], run, ident_f32[:])
@@ -102,8 +103,6 @@ def tile_dygcn_pb_t_e_kernel(
             )
             mx_tiles[r] = (codes, scales)
             b = r // ROUNDS_PER_BATCH
-            if r % ROUNDS_PER_BATCH == 0 and b + 1 < B:
-                sort_batch(b + 1)
             if (r + 1) % ROUNDS_PER_BATCH == 0 and b + X_BUFS < B:
                 load_batch(b + X_BUFS)
 
@@ -185,8 +184,8 @@ def tile_dygcn_pb_t_e_kernel(
         for b in range(1, X_BUFS):
             load_batch(b)
 
-        sort_batch(0)
-        for r in range(AHEAD):
+        sort_round(0)
+        for r in range(AHEAD - 1):
             transpose_round(r)
 
         same_tile = const.tile([P, CHUNK_TILES], F32, name="same_tile")
@@ -232,6 +231,8 @@ def tile_dygcn_pb_t_e_kernel(
             out=w_scales[:].bitcast(I32).rearrange("p j (e w) -> p j e w", w=O // 4),
             in_=w_scales_in[:].bitcast(I32).rearrange("p (e j w) -> p j e w", j=J, w=O // 4),
         )
+
+        transpose_round(AHEAD - 1)
 
         for r in range(ROUNDS):
             multiply_round(r)

from contextlib import ExitStack

import concourse.mybir as mybir
from concourse.masks import make_identity

BF16 = mybir.dt.bfloat16
F32 = mybir.dt.float32
I32 = mybir.dt.int32
U8 = mybir.dt.uint8
FP8X4 = mybir.dt.float8_e4m3fn_x4
MULT = mybir.AluOpType.mult
ADD = mybir.AluOpType.add

B, J, N, F, E, O = 16, 3, 512, 512, 16, 16
P = 128
PACK = 4
HALVES = 2
TILES = N // P
EO = E * O
BANK_UNITS = 2
BANK_TILES = 2
ROUND_UNITS = 4
ROUNDS_PER_BATCH = TILES * J // ROUND_UNITS
ROUNDS = B * ROUNDS_PER_BATCH
AHEAD = 3
X_BUFS = 4
SORTED_ORDERS = 1
CHUNK_TILES = P // E
CHUNKS = B * TILES // CHUNK_TILES

FLOPS = 2 * B * N * J * F * EO + 4 * B * N * EO


def tile_dygcn_pb_t_e_kernel(
    tc, x_g, emb, weights_pool_words, weights_pool_scales, bias_pool, out
):
    nc = tc.nc
    with ExitStack() as ctx:
        const = ctx.enter_context(tc.tile_pool(name="const", bufs=1))
        x_pool = ctx.enter_context(tc.tile_pool(name="x", bufs=X_BUFS))
        sort_pool = ctx.enter_context(tc.tile_pool(name="sort", bufs=6))
        stage = ctx.enter_context(tc.tile_pool(name="stage", bufs=3))
        mx_pool = ctx.enter_context(tc.tile_pool(name="mx", bufs=AHEAD + 2))
        psum_t = ctx.enter_context(tc.psum_pool(name="psum_t", bufs=6))
        psum_z = ctx.enter_context(tc.psum_pool(name="psum_z", bufs=2))
        ctx.enter_context(tc.manual_schedule())

        x_tiles = {}
        sorted_tiles = {}
        mx_tiles = {}
        z_tiles = {}
        res_tiles = {}

        def unit_of(r, k):
            tile_index, j = divmod(r * ROUND_UNITS + k, J)
            b, t = divmod(tile_index, TILES)
            return b, t, j

        def load_batch(b):
            x_sb = x_pool.tile([P, J, TILES, F], BF16, name="x_sb")
            for j in range(J):
                nc.sync.dma_start(
                    out=x_sb[:, j], in_=x_g[b, j].rearrange("(p t) f -> p t f", t=TILES)
                )
            x_tiles[b] = x_sb

        def sort_round(r):
            for k in range(ROUND_UNITS):
                b, t, j = unit_of(r, k)
                if j < SORTED_ORDERS:
                    runs = sort_pool.tile([P, HALVES, P], F32, name="runs")
                    nc.scalar.copy(
                        out=runs[:],
                        in_=x_tiles[b][:].bitcast(F32)[:, j, t].rearrange("p (q u) -> p u q", u=HALVES),
                    )
                    sorted_tiles[b, t, j] = runs

        def transpose_round(r):
            if r + 1 < ROUNDS:
                sort_round(r + 1)
            grouped = stage.tile([P, ROUND_UNITS, P, PACK], BF16, name="grouped", align_bytes=64)
            codes = mx_pool.tile([P, ROUND_UNITS * P], I32, name="codes", align_bytes=64)
            scales = mx_pool.tile([P, ROUND_UNITS * P], U8, name="scales", align_bytes=64)
            for first in range(0, ROUND_UNITS, BANK_UNITS):
                flipped = psum_t.tile([P, BANK_UNITS, HALVES, P], F32, name="flipped", tag="t")
                for i in range(BANK_UNITS):
                    b, t, j = unit_of(r, first + i)
                    words = x_tiles[b][:].bitcast(F32)
                    for u in range(HALVES):
                        if j < SORTED_ORDERS:
                            run = sorted_tiles[b, t, j][:, u, :]
                        else:
                            run = words[:, j, t, u : F // 2 : HALVES]
                        nc.tensor.transpose(flipped[:, i, u, :], run, ident_f32[:])
                nc.scalar.copy(
                    out=grouped[:].bitcast(F32)[:, first : first + BANK_UNITS],
                    in_=flipped[:].rearrange("p i u c -> p i c u"),
                )
            nc.vector.quantize_mx(
                out=codes[:].bitcast(FP8X4),
                scales=scales[:],
                in_=grouped[:].rearrange("p i c k -> p (i c k)"),
            )
            mx_tiles[r] = (codes, scales)
            b = r // ROUNDS_PER_BATCH
            if (r + 1) % ROUNDS_PER_BATCH == 0 and b + X_BUFS < B:
                load_batch(b + X_BUFS)

        def multiply_round(r):
            codes, scales = mx_tiles.pop(r)
            for k in range(ROUND_UNITS):
                b, t, j = unit_of(r, k)
                pair, side = divmod(t, BANK_TILES)
                if side == 0 and j == 0:
                    z_tiles[b, pair] = psum_z.tile([P, BANK_TILES, EO], F32, name="z", tag="z")
                nodes = slice(k * P, (k + 1) * P)
                nc.tensor.matmul_mx(
                    out=z_tiles[b, pair][:, side, :],
                    lhsT=codes[:, nodes].bitcast(FP8X4),
                    lhsT_scale=scales[:, nodes],
                    rhs=w_codes[:, j, :].bitcast(FP8X4),
                    rhs_scale=w_scales[:, j, :],
                    start=(j == 0),
                    stop=(j == J - 1),
                )
                if side == BANK_TILES - 1 and j == J - 1:
                    finish_pair(b, pair)

        def finish_pair(b, pair):
            tiles = slice(pair * BANK_TILES, (pair + 1) * BANK_TILES)
            weighted = stage.tile([P, BANK_TILES, O, E], F32, name="weighted")
            nc.vector.tensor_tensor(
                out=weighted[:],
                in0=z_tiles.pop((b, pair))[:].rearrange("p t (e o) -> p t o e", o=O),
                in1=emb_sb[:, b, tiles, :].unsqueeze(2).to_broadcast([P, BANK_TILES, O, E]),
                op=MULT,
            )
            if pair == 0:
                res_tiles[b] = stage.tile([P, TILES, O], F32, name="res")
            res = res_tiles[b]
            nc.vector.tensor_reduce(
                out=res[:, tiles, :], in_=weighted[:], axis=mybir.AxisListType.X, op=ADD
            )
            if (pair + 1) * BANK_TILES == TILES:
                nc.vector.tensor_tensor(out=res[:], in0=res[:], in1=bias_term[:, b], op=ADD)
                nc.sync.dma_start(
                    out=out[b].rearrange("(p t) o -> p t o", t=TILES), in_=res_tiles.pop(b)[:]
                )

        ident_f32 = const.tile([P, P], F32, name="ident_f32")
        make_identity(nc, ident_f32[:])
        ident_bf16 = const.tile([P, P], BF16, name="ident_bf16")
        make_identity(nc, ident_bf16[:])

        load_batch(0)

        emb_sb = const.tile([P, B, TILES, E], BF16, name="emb_sb")
        nc.sync.dma_start(out=emb_sb[:], in_=emb.rearrange("b (p t) e -> p b t e", t=TILES))
        bias_rows = const.tile([P, O], BF16, name="bias_rows")
        nc.sync.dma_start(
            out=bias_rows[:], in_=bias_pool.unsqueeze(0).to_broadcast([CHUNK_TILES, E, O])
        )

        w_scales_in = const.tile([P, E * J * O], U8, name="w_scales_in")
        nc.vector.memset(w_scales_in[:].bitcast(I32), 0)
        scale_rows = weights_pool_scales.bitcast(I32).rearrange("g (q r) w -> q r g w", r=4)
        for q in range(4):
            nc.sync.dma_start(
                out=w_scales_in[32 * q : 32 * q + 4, :]
                .bitcast(I32)
                .rearrange("r (g w) -> r g w", w=O // 4),
                in_=scale_rows[q],
            )
        w_codes = const.tile([P, J, EO], I32, name="w_codes", align_bytes=64)
        code_words = (
            weights_pool_words.rearrange("g p n t -> g p (n t)")
            .bitcast(I32)
            .rearrange("(e j) p n -> j p e n", j=J)
        )
        for j in range(J):
            nc.sync.dma_start(
                out=w_codes[:, j, :].rearrange("p (e n) -> p e n", n=O), in_=code_words[j]
            )
        for b in range(1, X_BUFS):
            load_batch(b)

        sort_round(0)
        for r in range(AHEAD - 1):
            transpose_round(r)

        same_tile = const.tile([P, CHUNK_TILES], F32, name="same_tile")
        nc.vector.tensor_reduce(
            out=same_tile[:],
            in_=ident_bf16[:].rearrange("p (i e) -> p i e", e=E),
            axis=mybir.AxisListType.X,
            op=ADD,
        )
        bias_blocks = const.tile([P, CHUNK_TILES, O], BF16, name="bias_blocks")
        nc.vector.tensor_tensor(
            out=bias_blocks[:],
            in0=bias_rows[:].unsqueeze(1).to_broadcast([P, CHUNK_TILES, O]),
            in1=same_tile[:].unsqueeze(2).to_broadcast([P, CHUNK_TILES, O]),
            op=MULT,
        )
        emb_cols = emb_sb[:].rearrange("p b t e -> p (b t e)")
        emb_flipped = psum_t.tile([P, CHUNKS, P], BF16, name="emb_flipped", tag="t")
        for c in range(CHUNKS):
            nc.tensor.transpose(emb_flipped[:, c, :], emb_cols[:, c * P : (c + 1) * P], ident_bf16[:])
        emb_t = const.tile([P, CHUNKS, P], BF16, name="emb_t")
        nc.vector.tensor_copy(out=emb_t[:], in_=emb_flipped[:])
        bias_term = const.tile([P, B, TILES, O], F32, name="bias_term")
        bias_term_cols = bias_term[:].rearrange("p b t o -> p (b t o)")
        bank_chunks = 512 // P
        for half in range(CHUNKS // bank_chunks):
            product = psum_z.tile([P, bank_chunks, P], F32, name="product", tag="z")
            for i in range(bank_chunks):
                nc.tensor.matmul(
                    out=product[:, i, :],
                    lhsT=emb_t[:, half * bank_chunks + i, :],
                    rhs=bias_blocks[:].rearrange("p i o -> p (i o)"),
                    start=True,
                    stop=True,
                )
            nc.vector.tensor_copy(
                out=bias_term_cols[:, half * 512 : (half + 1) * 512],
                in_=product[:].rearrange("p i c -> p (i c)"),
            )

        w_scales = const.tile([P, J, EO], U8, name="w_scales", align_bytes=64)
        nc.vector.tensor_copy(
            out=w_scales[:].bitcast(I32).rearrange("p j (e w) -> p j e w", w=O // 4),
            in_=w_scales_in[:].bitcast(I32).rearrange("p (e j w) -> p j e w", j=J, w=O // 4),
        )

        transpose_round(AHEAD - 1)

        for r in range(ROUNDS):
            multiply_round(r)
            if r + AHEAD < ROUNDS:
                transpose_round(r + AHEAD)
